import numpy as np
import ml_dtypes


def mxq(x, axis, fmt="e4m3"):
    dtype, down = {"e4m3": (ml_dtypes.float8_e4m3fn, 7), "e5m2": (ml_dtypes.float8_e5m2, 14)}[fmt]
    v = np.moveaxis(np.asarray(x, np.float32).astype(ml_dtypes.bfloat16).astype(np.float64), axis, -1)
    blocks = v.reshape(v.shape[:-1] + (-1, 32))
    amax = np.abs(blocks).max(-1, keepdims=True)
    byte = np.maximum(np.where(amax > 0, np.frexp(amax)[1] - 1 + 127, 0) - down, 1)
    scale = np.exp2(byte - 127.0)
    codes = (blocks / scale).astype(np.float32).astype(dtype).astype(np.float64)
    return np.moveaxis((codes * scale).reshape(v.shape), -1, axis)


WIDE = False


def mx_kscale(k):
    if not WIDE:
        return np.ones(k)
    levels = np.array([30, -30])
    if k % 512:
        return np.exp2(np.random.permutation(np.resize(levels, k // 32))).repeat(32)
    a = np.empty((k // 512, 16))
    for p in range(k // 512):
        a[p, :8] = np.random.permutation(np.resize(levels, 8))
        for g in range(8):
            far = levels[np.abs(levels - a[p, g]) >= 10]
            a[p, g + 8] = far[np.random.randint(len(far))]
    return np.exp2(a.ravel()).repeat(32)


BF16 = ml_dtypes.bfloat16


def bf(x):
    return np.asarray(x, np.float32).astype(BF16)


def f64(x):
    return np.asarray(x).astype(np.float64)


E2M1 = np.array([0.0, 0.5, 1.0, 1.5, 2.0, 3.0, 4.0, 6.0, -0.0, -0.5, -1.0, -1.5, -2.0, -3.0, -4.0, -6.0])


def pack_weight(w, fmt):
    k, n = w.shape
    w = f64(bf(w)).reshape(k // 32, 32, n)
    amax = np.abs(w).max(1)
    if fmt == "e4m3":
        byte = np.frexp(amax)[1] - 1 + 127 - 7
    else:
        mant, ex = np.frexp(amax / 6.0)
        byte = np.where(mant > 0.5, ex, ex - 1) + 127
    byte = np.clip(np.where(amax > 0, byte, 1), 1, 254)
    scaled = (w * np.exp2(127.0 - byte)[:, None, :]).reshape(k, n).astype(np.float32)
    by_word = np.ascontiguousarray(scaled.reshape(k // 512, 128, 4, n).transpose(0, 1, 3, 2))
    if fmt == "e4m3":
        words = by_word.astype(ml_dtypes.float8_e4m3fn).view(np.uint8)
    else:
        c = by_word.astype(ml_dtypes.float4_e2m1fn).view(np.uint8) & 0xF
        words = c[..., 0::2] | (c[..., 1::2] << 4)
    return np.ascontiguousarray(words), np.ascontiguousarray(byte.astype(np.uint8).reshape(k // 512, 16, n))


def unpack_weight(words, scales, fmt):
    g, p, n, _ = words.shape
    if fmt == "e4m3":
        vals = np.ascontiguousarray(words).view(ml_dtypes.float8_e4m3fn).astype(np.float64)
    else:
        nib = np.empty((g, p, n, 4), np.uint8)
        nib[..., 0::2] = words & 0xF
        nib[..., 1::2] = words >> 4
        vals = E2M1[nib]
    vals = vals * np.repeat(np.exp2(scales.astype(np.float64) - 127.0), 8, axis=1)[..., None]
    return vals.transpose(0, 1, 3, 2).reshape(g * 512, n)

def pack4(w):
    words, scales = pack_weight(w, "e2m1")
    return words.reshape(words.shape[0], 128, -1), scales


def unpack4(words, scales):
    return unpack_weight(words.reshape(words.shape[0], 128, -1, 2), scales, "e2m1")


S, HID, H, KV, D, WINDOW, QB = 1024, 1024, 8, 4, 256, 512, 512
NQ, NK = H * D, KV * D
EPS = 1e-6
ROPE_THETA = 10000.0


def rms_norm(x, w):
    var = np.mean(x * x, axis=-1, keepdims=True)
    return x * (1.0 / np.sqrt(var + EPS)) * (1.0 + w)


def rotate_half(x):
    x1, x2 = np.split(x, 2, axis=-1)
    return np.concatenate([-x2, x1], axis=-1)


def apply_rope(x, cos, sin):
    return x * cos[:, None, :] + rotate_half(x) * sin[:, None, :]


def setup_inputs():
    s = mx_kscale(HID)
    inv_freq = 1.0 / ROPE_THETA ** (np.arange(0, D, 2) / D)
    freqs = np.outer(np.arange(S), inv_freq)
    emb = np.concatenate([freqs, freqs], -1)
    hidden_states = bf(np.random.standard_normal((S, HID)) * s)
    words, scales = pack4(np.random.standard_normal((HID, NQ + NK + NK)) / np.sqrt(HID) / s[:, None])
    return {"hidden_states": hidden_states,
            "w_qkv_words": words, "w_qkv_scales": scales,
            "q_norm_w": bf(1.0 + 0.1 * np.random.standard_normal(D)),
            "k_norm_w": bf(1.0 + 0.1 * np.random.standard_normal(D)),
            "cos": bf(np.cos(emb)), "sin": bf(np.sin(emb))}


def reference(hidden_states, w_qkv_words, w_qkv_scales, q_norm_w, k_norm_w, cos, sin):
    qkv = mxq(f64(hidden_states), 1, "e5m2") @ unpack4(w_qkv_words, w_qkv_scales)
    q = qkv[:, :NQ].reshape(S, H, D)
    k = qkv[:, NQ:NQ + NK].reshape(S, KV, D)
    v = qkv[:, NQ + NK:].reshape(S, KV, D)
    q = rms_norm(q, f64(q_norm_w))
    k = rms_norm(k, f64(k_norm_w))
    q = apply_rope(q, f64(cos), f64(sin))
    k = apply_rope(k, f64(cos), f64(sin))
    return q, k, v

@@ -1,0 +1,286 @@
+from contextlib import ExitStack
+
+import concourse.mybir as mybir
+from concourse.masks import make_identity
+
+S, HID, H, KV, D = 1024, 1024, 8, 4, 256
+NQ, NK = H * D, KV * D
+N_ALL = NQ + 2 * NK
+EPS = 1e-6
+FLOPS = 2 * S * HID * N_ALL
+
+F32 = mybir.dt.float32
+BF16 = mybir.dt.bfloat16
+I32 = mybir.dt.int32
+U32 = mybir.dt.uint32
+U8 = mybir.dt.uint8
+FP8X4 = mybir.dt.float8_e5m2_x4
+FP4X4 = mybir.dt.float4_e2m1fn_x4
+ALU = mybir.AluOpType
+ACT = mybir.ActivationFunctionType
+
+P = 128
+HALF = D // 2
+PASSES = HID // 512
+BANK = 512
+TILES = S // P
+ROPE_BANKS = (NQ + NK) // BANK
+Q_BANKS = NQ // BANK
+UNIT = 2
+SQ_LEAD = 2
+MM_LEAD = 3
+EARLY_SCALE_COLS = NQ
+
+
+def tile_gemmaattention_pa_kernel(tc, hidden, w_words, w_scales, q_norm_w, k_norm_w, cos, sin, out_q, out_k, out_v):
+    nc = tc.nc
+    q_rows = out_q.rearrange("s h d -> s (h d)")
+    k_rows = out_k.rearrange("s h d -> s (h d)")
+    v_rows = out_v.rearrange("s h d -> s (h d)")
+    w_by_partition = w_words.rearrange("g p n -> p g n")
+
+    with ExitStack() as ctx:
+        keep = ctx.enter_context(tc.tile_pool(name="keep", bufs=1))
+        work = ctx.enter_context(tc.tile_pool(name="work", bufs=2))
+        aux_psum = ctx.enter_context(tc.psum_pool(name="aux_psum", bufs=1))
+        mx_psum = ctx.enter_context(tc.psum_pool(name="mx_psum", bufs=6))
+        ctx.enter_context(tc.manual_schedule())
+
+        x_tiles, cos_tiles, sin_tiles, w_chunks, w_planes = {}, {}, {}, {}, {}
+
+        def load_rows(dst, src, name, first, count):
+            width = src.shape[1]
+            tile = keep.tile([P, count, width], BF16, name="%s_%d" % (name, first))
+            rows = src[first * P:(first + count) * P, :]
+            nc.sync.dma_start(out=tile[:], in_=rows.rearrange("(t p) w -> p t w", p=P))
+            for i in range(count):
+                dst[first + i] = tile[:, i, :]
+
+        def load_weights(first, count):
+            tile = keep.tile([P, PASSES, 2 * BANK * count], U8, name="w_%d" % first, align_bytes=64)
+            src = w_by_partition[:, :, 2 * BANK * first:2 * BANK * (first + count)]
+            nc.sync.dma_start(out=tile[:].bitcast(I32), in_=src.bitcast(I32))
+            for i in range(count):
+                w_chunks[first + i] = tile[:, :, 2 * BANK * i:2 * BANK * (i + 1)]
+
+        def load_scales(col0, col1):
+            plane = keep.tile([P, PASSES, col1 - col0], U8, name="w_scale_%d" % col0, align_bytes=64)
+            for quad in range(4):
+                src = w_scales[:, 4 * quad:4 * quad + 4, col0:col1].rearrange("g r n -> r g n")
+                nc.sync.dma_start(out=plane[32 * quad:32 * quad + 4, :, :].bitcast(I32), in_=src.bitcast(I32))
+            for c in range(col0 // BANK, col1 // BANK):
+                w_planes[c] = plane[:, :, c * BANK - col0:(c + 1) * BANK - col0]
+
+        ident = keep.tile([P, P], F32)
+        make_identity(nc, ident[:])
+        norm_row = keep.tile([P, 2, D], BF16)
+        nc.vector.memset(norm_row[:], 0.0)
+        nc.gpsimd.dma_start(out=norm_row[0:1, 0, :], in_=q_norm_w.unsqueeze(0))
+        nc.gpsimd.dma_start(out=norm_row[0:1, 1, :], in_=k_norm_w.unsqueeze(0))
+        ones = keep.tile([P, P], BF16)
+        nc.vector.memset(ones[:], 1.0)
+
+        load_rows(x_tiles, hidden, "x", 0, 1)
+        load_rows(cos_tiles, cos, "cos", 0, 1)
+        load_rows(sin_tiles, sin, "sin", 0, 1)
+        load_scales(0, EARLY_SCALE_COLS)
+        load_weights(0, 1)
+        load_weights(1, 1)
+        load_weights(2, 1)
+        load_rows(x_tiles, hidden, "x", 1, 1)
+        load_rows(cos_tiles, cos, "cos", 1, 1)
+        load_rows(sin_tiles, sin, "sin", 1, 1)
+        load_weights(3, 1)
+        load_scales(EARLY_SCALE_COLS, N_ALL)
+        load_weights(4, 2)
+        load_weights(6, 2)
+        load_rows(x_tiles, hidden, "x", 2, 2)
+        load_rows(cos_tiles, cos, "cos", 2, TILES - 2)
+        load_rows(sin_tiles, sin, "sin", 2, TILES - 2)
+        load_rows(x_tiles, hidden, "x", 4, TILES - 4)
+
+        eye_pair = keep.tile([P, 2, P], BF16)
+        neg_eye_pair = keep.tile([P, 2, P], BF16)
+        for i in range(2):
+            nc.vector.tensor_copy(out=eye_pair[:, i, :], in_=ident[:])
+        nc.vector.tensor_scalar(out=neg_eye_pair[:], in0=eye_pair[:], scalar1=-1.0, scalar2=None, op0=ALU.mult)
+
+        xt_banks, cst_banks, grouped, codes, scales, cs_t, table_banks, tables = {}, {}, {}, {}, {}, {}, {}, {}
+        banks, sums, rstd, direct, crossed, v_banks, v_tiles = {}, {}, {}, {}, {}, {}, {}
+
+        def transpose_x(t):
+            words = x_tiles[t].bitcast(F32)
+            xt = aux_psum.tile([P, PASSES, 2, P], F32, name="aux_a")
+            for g in range(PASSES):
+                for u in range(2):
+                    nc.tensor.transpose(xt[:, g, u, :], words[:, 256 * g + u:256 * (g + 1):2], ident[:])
+            xt_banks[t] = xt
+
+        def transpose_cos_sin(t):
+            cst = aux_psum.tile([P, 2, 2, P], BF16, name="aux_b")
+            for i, src in enumerate((cos_tiles[t], sin_tiles[t])):
+                for hf in range(2):
+                    nc.tensor.transpose(cst[:, i, hf, :], src[:, hf * HALF:(hf + 1) * HALF], eye_pair[:, 0, :])
+            cst_banks[t] = cst
+
+        def copy_x(t):
+            tile = work.tile([P, PASSES, P, 2], F32, name="grouped", align_bytes=64)
+            nc.scalar.copy(out=tile[:], in_=xt_banks[t][:].rearrange("p g u r -> p g r u"))
+            grouped[t] = tile
+
+        def quantize_x(t):
+            codes[t] = work.tile([P, PASSES * P], U32, name="codes", align_bytes=64)
+            scales[t] = work.tile([P, PASSES * P], U8, name="scales", align_bytes=64)
+            nc.vector.quantize_mx(
+                out=codes[t][:].bitcast(FP8X4),
+                scales=scales[t][:],
+                in_=grouped[t][:].rearrange("p g r u -> p (g r u)").bitcast(BF16),
+            )
+
+        def copy_cos_sin(t):
+            cs_t[t] = work.tile([P, 2, 2, P], BF16, name="cs_t")
+            nc.scalar.copy(out=cs_t[t][:], in_=cst_banks[t][:])
+
+        def multiply_tables(t):
+            for i, tag in enumerate(("aux_a", "aux_b")):
+                bank = aux_psum.tile([P, 2, 2 * P], F32, name=tag)
+                for hf in range(2):
+                    gain, one = table_factors[i][hf]
+                    nc.tensor.matmul(bank[:, hf, :], lhsT=cs_t[t][:, i, hf, :], rhs=gain, start=True, stop=False)
+                    nc.tensor.matmul(bank[:, hf, :], lhsT=cs_t[t][:, i, hf, :], rhs=one, start=False, stop=True)
+                table_banks[t, i] = bank
+
+        def copy_table(t, i):
+            tile = work.tile([P, 2, 2, HALF], F32, name="table_%d" % i)
+            nc.scalar.copy(out=tile[:].rearrange("p a b c -> p (a b c)"), in_=table_banks[t, i][:].rearrange("p a b -> p (a b)"))
+            tables[t, i] = tile
+
+        def project(t, chunk):
+            bank = mx_psum.tile([P, BANK], F32, name="mx_bank")
+            for g in range(PASSES):
+                nc.tensor.matmul_mx(
+                    out=bank[:],
+                    lhsT=codes[t][:, g * P:(g + 1) * P].bitcast(FP8X4),
+                    lhsT_scale=scales[t][:, g * P:(g + 1) * P],
+                    rhs=w_chunks[chunk][:, g, :].bitcast(FP4X4),
+                    rhs_scale=w_planes[chunk][:, g, :],
+                    start=(g == 0),
+                    stop=(g == PASSES - 1),
+                )
+            return bank
+
+        def project_rope_bank(s):
+            banks[s] = project(s // ROPE_BANKS, s % ROPE_BANKS)
+
+        def square_sums(s):
+            sums[s] = work.tile([P, 2], F32, name="sums", bufs=4)
+            for h in range(2):
+                squares = work.tile([P, D], BF16, name="squares")
+                nc.scalar.activation(out=squares[:], in_=banks[s][:, h * D:(h + 1) * D], func=ACT.Square, accum_out=sums[s][:, h:h + 1])
+
+        def inverse_rms(s):
+            rstd[s] = work.tile([P, 2], F32, name="rstd", bufs=4)
+            nc.scalar.activation(out=rstd[s][:], in_=sums[s][:], func=ACT.Abs_reciprocal_sqrt, scale=1.0 / D, bias=EPS)
+
+        def rope_products(s):
+            t, j = divmod(s, ROPE_BANKS)
+            unit = s // UNIT
+            if s % UNIT == 0:
+                direct[unit] = work.tile([P, UNIT * BANK], F32, name="direct", bufs=4)
+                crossed[unit] = work.tile([P, UNIT * BANK], F32, name="crossed", bufs=3)
+            which = 0 if j < Q_BANKS else 1
+            for h in range(2):
+                head = banks[s][:, h * D:(h + 1) * D].rearrange("p (a b) -> p a b", a=2)
+                cols = slice((s % UNIT) * BANK + h * D, (s % UNIT) * BANK + (h + 1) * D)
+                for dst, src, i in ((direct, head, 0), (crossed, head[:, ::-1, :], 1)):
+                    nc.vector.scalar_tensor_tensor(
+                        out=dst[unit][:, cols].rearrange("p (a b) -> p a b", a=2),
+                        in0=src,
+                        scalar=rstd[s][:, h:h + 1],
+                        in1=tables[t, i][:, :, which, :],
+                        op0=ALU.mult,
+                        op1=ALU.mult,
+                    )
+
+        def add_and_store(engine, unit, col0, col1):
+            t, j = divmod(unit * UNIT, ROPE_BANKS)
+            y = direct[unit][:, col0:col1]
+            engine.tensor_tensor(out=y, in0=y, in1=crossed[unit][:, col0:col1], op=ALU.add)
+            dst, first = (q_rows, j * BANK) if j < Q_BANKS else (k_rows, (j - Q_BANKS) * BANK)
+            nc.sync.dma_start(out=dst[t * P:(t + 1) * P, first + col0:first + col1], in_=y)
+
+        def project_v(t, i):
+            v_banks[t, i] = project(t, ROPE_BANKS + i)
+
+        def copy_v(t, i):
+            if i == 0:
+                v_tiles[t] = work.tile([P, NK], F32, name="v_tile")
+            nc.scalar.copy(out=v_tiles[t][:, i * BANK:(i + 1) * BANK], in_=v_banks[t, i][:])
+            if i == 1:
+                nc.sync.dma_start(out=v_rows[t * P:(t + 1) * P, :], in_=v_tiles[t][:])
+
+        transpose_x(0)
+        copy_x(0)
+        norm_bank = mx_psum.tile([P, 2, 2, HALF], F32, name="mx_bank")
+        nc.tensor.matmul(norm_bank[:].rearrange("p a b c -> p (a b c)"), lhsT=ones[:], rhs=norm_row[:].rearrange("p a d -> p (a d)"), start=True, stop=True)
+        transpose_cos_sin(0)
+        copy_cos_sin(0)
+        diag = keep.tile([P, 2, 2, HALF], BF16)
+        neg_diag = keep.tile([P, 2, HALF], BF16)
+        for hf in range(2):
+            nc.vector.tensor_tensor(out=diag[:, hf, :, :], in0=norm_bank[:, :, hf, :], in1=eye_pair[:], op=ALU.mult)
+        nc.vector.tensor_tensor(out=neg_diag[:], in0=norm_bank[:, :, 1, :], in1=neg_eye_pair[:], op=ALU.mult)
+        flat = lambda ap: ap.rearrange("p a b -> p (a b)")
+        plus, minus = flat(eye_pair[:]), flat(neg_eye_pair[:])
+        table_factors = (
+            ((flat(diag[:, 0, :, :]), plus), (flat(diag[:, 1, :, :]), plus)),
+            ((flat(neg_diag[:]), minus), (flat(diag[:, 0, :, :]), plus)),
+        )
+        quantize_x(0)
+        multiply_tables(0)
+        project_rope_bank(0)
+        copy_table(0, 0)
+        square_sums(0)
+        project_rope_bank(1)
+        copy_table(0, 1)
+        inverse_rms(0)
+        square_sums(1)
+        project_rope_bank(2)
+        inverse_rms(1)
+
+        steps = TILES * ROPE_BANKS
+        for s in range(steps):
+            t, j = divmod(s, ROPE_BANKS)
+            last_tile = t == TILES - 1
+            v_first = 0 if last_tile else 4
+            if j == 0 and not last_tile:
+                transpose_x(t + 1)
+                transpose_cos_sin(t + 1)
+            if j == 2 and not last_tile:
+                multiply_tables(t + 1)
+            if j - v_first in (0, 1):
+                project_v(t, j - v_first)
+            if s + MM_LEAD < steps:
+                project_rope_bank(s + MM_LEAD)
+            if s + SQ_LEAD < steps:
+                square_sums(s + SQ_LEAD)
+            if not last_tile:
+                if j == 0:
+                    copy_x(t + 1)
+                if j == 1:
+                    copy_cos_sin(t + 1)
+                if j in (2, 3):
+                    copy_table(t + 1, j - 2)
+            if j - v_first in (0, 1):
+                copy_v(t, j - v_first)
+            if s + SQ_LEAD < steps:
+                inverse_rms(s + SQ_LEAD)
+            rope_products(s)
+            if j == 1 and not last_tile:
+                quantize_x(t + 1)
+            if s % UNIT == UNIT - 1:
+                if s < steps - 1:
+                    add_and_store(nc.gpsimd, s // UNIT, 0, UNIT * BANK)
+                else:
+                    for b in range(UNIT):
+                        add_and_store(nc.vector, s // UNIT, b * BANK, (b + 1) * BANK)

@@ -28,7 +28,11 @@ ROPE_BANKS = (NQ + NK) // BANK
 Q_BANKS = NQ // BANK
 UNIT = 2
 SQ_LEAD = 2
-MM_LEAD = 3
+MM_LEAD = 4
+PREP_LEAD = 8
+V_STEP = 8
+STORE_LAG = 1
+V_END = 4
 EARLY_SCALE_COLS = NQ
 
 
@@ -71,26 +75,22 @@ def tile_gemmaattention_pa_kernel(tc, hidden, w_words, w_scales, q_norm_w, k_nor
             for c in range(col0 // BANK, col1 // BANK):
                 w_planes[c] = plane[:, :, c * BANK - col0:(c + 1) * BANK - col0]
 
-        ident = keep.tile([P, P], F32)
-        make_identity(nc, ident[:])
         norm_row = keep.tile([P, 2, D], BF16)
         nc.vector.memset(norm_row[:], 0.0)
-        nc.gpsimd.dma_start(out=norm_row[0:1, 0, :], in_=q_norm_w.unsqueeze(0))
-        nc.gpsimd.dma_start(out=norm_row[0:1, 1, :], in_=k_norm_w.unsqueeze(0))
+        ident = keep.tile([P, P], F32)
+        make_identity(nc, ident[:])
         ones = keep.tile([P, P], BF16)
         nc.vector.memset(ones[:], 1.0)
 
         load_rows(x_tiles, hidden, "x", 0, 1)
-        load_rows(cos_tiles, cos, "cos", 0, 1)
-        load_rows(sin_tiles, sin, "sin", 0, 1)
         load_scales(0, EARLY_SCALE_COLS)
-        load_weights(0, 1)
-        load_weights(1, 1)
-        load_weights(2, 1)
+        load_weights(0, 2)
+        nc.sync.dma_start(out=norm_row[0:1, 0, :], in_=q_norm_w.unsqueeze(0))
+        nc.sync.dma_start(out=norm_row[0:1, 1, :], in_=k_norm_w.unsqueeze(0))
+        load_rows(cos_tiles, cos, "cos", 0, 2)
+        load_rows(sin_tiles, sin, "sin", 0, 2)
         load_rows(x_tiles, hidden, "x", 1, 1)
-        load_rows(cos_tiles, cos, "cos", 1, 1)
-        load_rows(sin_tiles, sin, "sin", 1, 1)
-        load_weights(3, 1)
+        load_weights(2, 2)
         load_scales(EARLY_SCALE_COLS, N_ALL)
         load_weights(4, 2)
         load_weights(6, 2)
@@ -106,7 +106,9 @@ def tile_gemmaattention_pa_kernel(tc, hidden, w_words, w_scales, q_norm_w, k_nor
         nc.vector.tensor_scalar(out=neg_eye_pair[:], in0=eye_pair[:], scalar1=-1.0, scalar2=None, op0=ALU.mult)
 
         xt_banks, cst_banks, grouped, codes, scales, cs_t, table_banks, tables = {}, {}, {}, {}, {}, {}, {}, {}
-        banks, sums, rstd, direct, crossed, v_banks, v_tiles = {}, {}, {}, {}, {}, {}, {}
+        heads, sums, rstd, products, v_banks, v_tiles = {}, {}, {}, {}, {}, {}
+
+        unstored = []
 
         def transpose_x(t):
             words = x_tiles[t].bitcast(F32)
@@ -123,14 +125,14 @@ def tile_gemmaattention_pa_kernel(tc, hidden, w_words, w_scales, q_norm_w, k_nor
                     nc.tensor.transpose(cst[:, i, hf, :], src[:, hf * HALF:(hf + 1) * HALF], eye_pair[:, 0, :])
             cst_banks[t] = cst
 
-        def copy_x(t):
+        def copy_x(t, copy):
             tile = work.tile([P, PASSES, P, 2], F32, name="grouped", align_bytes=64)
-            nc.scalar.copy(out=tile[:], in_=xt_banks[t][:].rearrange("p g u r -> p g r u"))
+            copy(out=tile[:], in_=xt_banks[t][:].rearrange("p g u r -> p g r u"))
             grouped[t] = tile
 
         def quantize_x(t):
-            codes[t] = work.tile([P, PASSES * P], U32, name="codes", align_bytes=64)
-            scales[t] = work.tile([P, PASSES * P], U8, name="scales", align_bytes=64)
+            codes[t] = work.tile([P, PASSES * P], U32, name="codes", bufs=3, align_bytes=64)
+            scales[t] = work.tile([P, PASSES * P], U8, name="scales", bufs=3, align_bytes=64)
             nc.vector.quantize_mx(
                 out=codes[t][:].bitcast(FP8X4),
                 scales=scales[t][:],
@@ -146,141 +148,180 @@ def tile_gemmaattention_pa_kernel(tc, hidden, w_words, w_scales, q_norm_w, k_nor
                 bank = aux_psum.tile([P, 2, 2 * P], F32, name=tag)
                 for hf in range(2):
                     gain, one = table_factors[i][hf]
-                    nc.tensor.matmul(bank[:, hf, :], lhsT=cs_t[t][:, i, hf, :], rhs=gain, start=True, stop=False)
-                    nc.tensor.matmul(bank[:, hf, :], lhsT=cs_t[t][:, i, hf, :], rhs=one, start=False, stop=True)
+                    angles = cs_t[t][:, i, hf if i == 0 else 1 - hf, :]
+                    nc.tensor.matmul(bank[:, hf, :], lhsT=angles, rhs=gain, start=True, stop=False)
+                    nc.tensor.matmul(bank[:, hf, :], lhsT=angles, rhs=one, start=False, stop=True)
                 table_banks[t, i] = bank
 
         def copy_table(t, i):
-            tile = work.tile([P, 2, 2, HALF], F32, name="table_%d" % i)
-            nc.scalar.copy(out=tile[:].rearrange("p a b c -> p (a b c)"), in_=table_banks[t, i][:].rearrange("p a b -> p (a b)"))
-            tables[t, i] = tile
+            if i == 0:
+                tables[t] = work.tile([P, 2, 2, 2, HALF], F32, name="table", bufs=3)
+            nc.scalar.copy(out=tables[t][:, i, :, :, :].rearrange("p a b c -> p (a b c)"), in_=table_banks[t, i][:].rearrange("p a b -> p (a b)"))
 
-        def project(t, chunk):
-            bank = mx_psum.tile([P, BANK], F32, name="mx_bank")
+        def project(bank, t, chunk, col0=0, col1=BANK):
             for g in range(PASSES):
                 nc.tensor.matmul_mx(
                     out=bank[:],
                     lhsT=codes[t][:, g * P:(g + 1) * P].bitcast(FP8X4),
                     lhsT_scale=scales[t][:, g * P:(g + 1) * P],
-                    rhs=w_chunks[chunk][:, g, :].bitcast(FP4X4),
-                    rhs_scale=w_planes[chunk][:, g, :],
+                    rhs=w_chunks[chunk][:, g, 2 * col0:2 * col1].bitcast(FP4X4),
+                    rhs_scale=w_planes[chunk][:, g, col0:col1],
                     start=(g == 0),
                     stop=(g == PASSES - 1),
                 )
             return bank
 
         def project_rope_bank(s):
-            banks[s] = project(s // ROPE_BANKS, s % ROPE_BANKS)
+            t, chunk = divmod(s, ROPE_BANKS)
+            if s == 0:
+                heads[s] = []
+                for h in range(2):
+                    bank = mx_psum.tile([P, D], F32, name="mx_bank")
+                    heads[s].append(project(bank, t, chunk, h * D, (h + 1) * D)[:])
+            else:
+                bank = mx_psum.tile([P, BANK], F32, name="mx_bank")
+                project(bank, t, chunk)
+                heads[s] = [bank[:, :D], bank[:, D:]]
 
-        def square_sums(s):
-            sums[s] = work.tile([P, 2], F32, name="sums", bufs=4)
-            for h in range(2):
-                squares = work.tile([P, D], BF16, name="squares")
-                nc.scalar.activation(out=squares[:], in_=banks[s][:, h * D:(h + 1) * D], func=ACT.Square, accum_out=sums[s][:, h:h + 1])
+        def square_sum(s, h):
+            unit, col = s // UNIT, 2 * (s % UNIT) + h
+            if col == 0:
+                sums[unit] = work.tile([P, 2 * UNIT], F32, name="sums", bufs=3)
+                rstd[unit] = work.tile([P, 2 * UNIT], F32, name="rstd", bufs=3)
+            squares = work.tile([P, D], BF16, name="squares")
+            nc.scalar.activation(out=squares[:], in_=heads[s][h], func=ACT.Square, accum_out=sums[unit][:, col:col + 1])
 
-        def inverse_rms(s):
-            rstd[s] = work.tile([P, 2], F32, name="rstd", bufs=4)
-            nc.scalar.activation(out=rstd[s][:], in_=sums[s][:], func=ACT.Abs_reciprocal_sqrt, scale=1.0 / D, bias=EPS)
+        def inverse_rms(unit, col0, col1):
+            nc.scalar.activation(out=rstd[unit][:, col0:col1], in_=sums[unit][:, col0:col1], func=ACT.Abs_reciprocal_sqrt, scale=1.0 / D, bias=EPS)
 
-        def rope_products(s):
+        def rope_products(s, h):
             t, j = divmod(s, ROPE_BANKS)
-            unit = s // UNIT
-            if s % UNIT == 0:
-                direct[unit] = work.tile([P, UNIT * BANK], F32, name="direct", bufs=4)
-                crossed[unit] = work.tile([P, UNIT * BANK], F32, name="crossed", bufs=3)
-            which = 0 if j < Q_BANKS else 1
-            for h in range(2):
-                head = banks[s][:, h * D:(h + 1) * D].rearrange("p (a b) -> p a b", a=2)
-                cols = slice((s % UNIT) * BANK + h * D, (s % UNIT) * BANK + (h + 1) * D)
-                for dst, src, i in ((direct, head, 0), (crossed, head[:, ::-1, :], 1)):
-                    nc.vector.scalar_tensor_tensor(
-                        out=dst[unit][:, cols].rearrange("p (a b) -> p a b", a=2),
-                        in0=src,
-                        scalar=rstd[s][:, h:h + 1],
-                        in1=tables[t, i][:, :, which, :],
-                        op0=ALU.mult,
-                        op1=ALU.mult,
-                    )
+            unit, col = s // UNIT, 2 * (s % UNIT) + h
+            if col == 0:
+                products[unit] = work.tile([P, 2 * UNIT, 2, 2, HALF], F32, name="products", bufs=3)
+            head = heads[s][h].rearrange("p (a b) -> p a b", a=2)
+            nc.vector.scalar_tensor_tensor(
+                out=products[unit][:, col, :, :, :],
+                in0=head.unsqueeze(1).broadcast_to([P, 2, 2, HALF]),
+                scalar=rstd[unit][:, col:col + 1],
+                in1=tables[t][:, :, :, 0 if j < Q_BANKS else 1, :],
+                op0=ALU.mult,
+                op1=ALU.mult,
+            )
 
-        def add_and_store(engine, unit, col0, col1):
+        def add_products(engine, unit, head0, head1):
+            y = work.tile([P, head1 - head0, 2, HALF], F32, name="y", bufs=6)
+            engine.tensor_tensor(out=y[:], in0=products[unit][:, head0:head1, 0, :, :], in1=products[unit][:, head0:head1, 1, ::-1, :], op=ALU.add)
+            unstored.append((y, unit, head0, head1))
+
+        def store_oldest():
+            y, unit, head0, head1 = unstored.pop(0)
             t, j = divmod(unit * UNIT, ROPE_BANKS)
-            y = direct[unit][:, col0:col1]
-            engine.tensor_tensor(out=y, in0=y, in1=crossed[unit][:, col0:col1], op=ALU.add)
             dst, first = (q_rows, j * BANK) if j < Q_BANKS else (k_rows, (j - Q_BANKS) * BANK)
-            nc.sync.dma_start(out=dst[t * P:(t + 1) * P, first + col0:first + col1], in_=y)
+            nc.sync.dma_start(out=dst[t * P:(t + 1) * P, first + head0 * D:first + head1 * D], in_=y[:].rearrange("p h a b -> p (h a b)"))
 
         def project_v(t, i):
-            v_banks[t, i] = project(t, ROPE_BANKS + i)
+            bank = aux_psum.tile([P, BANK], F32, name=("aux_a", "aux_b")[i])
+            v_banks[t, i] = project(bank, t, ROPE_BANKS + i)
 
         def copy_v(t, i):
             if i == 0:
-                v_tiles[t] = work.tile([P, NK], F32, name="v_tile")
+                v_tiles[t] = work.tile([P, NK], F32, name="v_tile", bufs=3)
             nc.scalar.copy(out=v_tiles[t][:, i * BANK:(i + 1) * BANK], in_=v_banks[t, i][:])
             if i == 1:
                 nc.sync.dma_start(out=v_rows[t * P:(t + 1) * P, :], in_=v_tiles[t][:])
 
         transpose_x(0)
-        copy_x(0)
+        copy_x(0, nc.scalar.copy)
         norm_bank = mx_psum.tile([P, 2, 2, HALF], F32, name="mx_bank")
         nc.tensor.matmul(norm_bank[:].rearrange("p a b c -> p (a b c)"), lhsT=ones[:], rhs=norm_row[:].rearrange("p a d -> p (a d)"), start=True, stop=True)
-        transpose_cos_sin(0)
-        copy_cos_sin(0)
+        quantize_x(0)
+        norm_all = keep.tile([P, 2, 2, HALF], BF16)
+        nc.scalar.copy(out=norm_all[:], in_=norm_bank[:])
+        neg_sin = keep.tile([P, HALF], BF16)
+        nc.scalar.activation(out=neg_sin[:], in_=sin_tiles[0][:, :HALF], func=ACT.Copy, scale=-1.0)
         diag = keep.tile([P, 2, 2, HALF], BF16)
         neg_diag = keep.tile([P, 2, HALF], BF16)
         for hf in range(2):
-            nc.vector.tensor_tensor(out=diag[:, hf, :, :], in0=norm_bank[:, :, hf, :], in1=eye_pair[:], op=ALU.mult)
-        nc.vector.tensor_tensor(out=neg_diag[:], in0=norm_bank[:, :, 1, :], in1=neg_eye_pair[:], op=ALU.mult)
+            nc.gpsimd.tensor_tensor(out=diag[:, hf, :, :], in0=norm_all[:, :, hf, :], in1=eye_pair[:], op=ALU.mult)
+        nc.gpsimd.tensor_tensor(out=neg_diag[:], in0=norm_all[:, :, 1, :], in1=neg_eye_pair[:], op=ALU.mult)
         flat = lambda ap: ap.rearrange("p a b -> p (a b)")
         plus, minus = flat(eye_pair[:]), flat(neg_eye_pair[:])
         table_factors = (
             ((flat(diag[:, 0, :, :]), plus), (flat(diag[:, 1, :, :]), plus)),
-            ((flat(neg_diag[:]), minus), (flat(diag[:, 0, :, :]), plus)),
+            ((flat(diag[:, 0, :, :]), plus), (flat(neg_diag[:]), minus)),
         )
-        quantize_x(0)
-        multiply_tables(0)
-        project_rope_bank(0)
-        copy_table(0, 0)
-        square_sums(0)
-        project_rope_bank(1)
-        copy_table(0, 1)
-        inverse_rms(0)
-        square_sums(1)
-        project_rope_bank(2)
-        inverse_rms(1)
+        tables[0] = work.tile([P, 2, 2, 2, HALF], F32, name="table", bufs=3)
+
+        def first_tables(which):
+            parts = (
+                (tables[0][:, 0, :, which, :], norm_bank[:, which, :, :], cos_tiles[0].rearrange("p (a b) -> p a b", a=2)),
+                (tables[0][:, 1, 0, which, :], norm_bank[:, which, 0, :], sin_tiles[0][:, HALF:]),
+                (tables[0][:, 1, 1, which, :], norm_bank[:, which, 1, :], neg_sin[:]),
+            )
+            for dst, weight, angles in parts:
+                nc.vector.scalar_tensor_tensor(out=dst, in0=weight, scalar=1.0, in1=angles, op0=ALU.add, op1=ALU.mult)
+
+        first_tables(0)
+        for s in range(MM_LEAD):
+            if s == UNIT:
+                transpose_x(1)
+                transpose_cos_sin(1)
+            project_rope_bank(s)
+        for col in range(2 * UNIT):
+            square_sum(col // 2, col % 2)
+            if col in (0, 1):
+                inverse_rms(0, col, col + 1)
+        inverse_rms(0, 2, 2 * UNIT)
 
         steps = TILES * ROPE_BANKS
+        prep_start = {max(u * ROPE_BANKS - PREP_LEAD, 0): u for u in range(1, TILES)}
+        v_start = {min(t * ROPE_BANKS + V_STEP, steps - V_END - 2 * (TILES - 1 - t)): t for t in range(TILES)}
         for s in range(steps):
-            t, j = divmod(s, ROPE_BANKS)
-            last_tile = t == TILES - 1
-            v_first = 0 if last_tile else 4
-            if j == 0 and not last_tile:
-                transpose_x(t + 1)
-                transpose_cos_sin(t + 1)
-            if j == 2 and not last_tile:
-                multiply_tables(t + 1)
-            if j - v_first in (0, 1):
-                project_v(t, j - v_first)
+            if s in prep_start and s > 0:
+                transpose_x(prep_start[s])
+                transpose_cos_sin(prep_start[s])
+            if s - 2 in prep_start:
+                multiply_tables(prep_start[s - 2])
+            for i in range(2):
+                if s - i in v_start:
+                    project_v(v_start[s - i], i)
             if s + MM_LEAD < steps:
                 project_rope_bank(s + MM_LEAD)
-            if s + SQ_LEAD < steps:
-                square_sums(s + SQ_LEAD)
-            if not last_tile:
-                if j == 0:
-                    copy_x(t + 1)
-                if j == 1:
-                    copy_cos_sin(t + 1)
-                if j in (2, 3):
-                    copy_table(t + 1, j - 2)
-            if j - v_first in (0, 1):
-                copy_v(t, j - v_first)
-            if s + SQ_LEAD < steps:
-                inverse_rms(s + SQ_LEAD)
-            rope_products(s)
-            if j == 1 and not last_tile:
-                quantize_x(t + 1)
+            ahead = s + SQ_LEAD
+            if ahead < steps:
+                for h in range(2):
+                    square_sum(ahead, h)
+            if s in prep_start and s > 0:
+                copy_x(prep_start[s], nc.scalar.copy)
+            if s - 1 in prep_start:
+                copy_cos_sin(prep_start[s - 1])
+            for i in range(2):
+                if s - 2 - i in prep_start:
+                    copy_table(prep_start[s - 2 - i], i)
+                if s - i in v_start:
+                    copy_v(v_start[s - i], i)
+            if ahead < steps and ahead % UNIT == UNIT - 1:
+                inverse_rms(ahead // UNIT, 0, 2 * UNIT)
+            rope_products(s, 0)
+            if s == 1:
+                quantize_x(1)
+            rope_products(s, 1)
+            if s == 0:
+                copy_x(1, nc.vector.tensor_copy)
+                first_tables(1)
+            if s - 1 in prep_start and s > 1:
+                quantize_x(prep_start[s - 1])
             if s % UNIT == UNIT - 1:
-                if s < steps - 1:
-                    add_and_store(nc.gpsimd, s // UNIT, 0, UNIT * BANK)
-                else:
+                if s < steps - 1 - UNIT:
+                    add_products(nc.gpsimd, s // UNIT, 0, 2 * UNIT)
+                    if len(unstored) > STORE_LAG:
+                        store_oldest()
+                elif s < steps - 1:
                     for b in range(UNIT):
-                        add_and_store(nc.vector, s // UNIT, b * BANK, (b + 1) * BANK)
+                        add_products(nc.gpsimd, s // UNIT, 2 * b, 2 * b + 2)
+                else:
+                    for head0, head1 in ((0, 2), (2, 3), (3, 4)):
+                        add_products(nc.vector, s // UNIT, head0, head1)
+        while unstored:
+            store_oldest()

@@ -82,6 +82,9 @@ def tile_gemmaattention_pa_kernel(tc, hidden, w_words, w_scales, q_norm_w, k_nor
         ones = keep.tile([P, P], BF16)
         nc.vector.memset(ones[:], 1.0)
 
+        warm = keep.tile([P, 1], F32)
+        nc.scalar.activation(out=warm[:], in_=ones[:, 0:1], func=ACT.Abs_reciprocal_sqrt)
+
         load_rows(x_tiles, hidden, "x", 0, 1)
         load_scales(0, EARLY_SCALE_COLS)
         load_weights(0, 2)

@@ -21,19 +21,30 @@ ACT = mybir.ActivationFunctionType
 
 P = 128
 HALF = D // 2
-PASSES = HID // 512
+K_PASS = 512
+PASSES = HID // K_PASS
+PASS_WORDS = K_PASS // 2
 BANK = 512
 TILES = S // P
-ROPE_BANKS = (NQ + NK) // BANK
-Q_BANKS = NQ // BANK
+TILE_STEPS = (NQ + NK) // BANK
+Q_STEPS = NQ // BANK
+STEPS = TILES * TILE_STEPS
 UNIT = 2
-SQ_LEAD = 2
-MM_LEAD = 4
+UNIT_HEADS = 2 * UNIT
+
+SQUARE_LEAD = 2
+MATMUL_LEAD = 4
 PREP_LEAD = 8
-V_STEP = 8
-STORE_LAG = 1
+V_DELAY = 8
 V_END = 4
-EARLY_SCALE_COLS = NQ
+STORE_LAG = 1
+
+MX_BANKS = 6
+AUX_BANKS = ("aux_a", "aux_b")
+
+
+def flat(ap):
+    return ap.rearrange("p a b -> p (a b)")
 
 
 def tile_gemmaattention_pa_kernel(tc, hidden, w_words, w_scales, q_norm_w, k_norm_w, cos, sin, out_q, out_k, out_v):
@@ -47,10 +58,10 @@ def tile_gemmaattention_pa_kernel(tc, hidden, w_words, w_scales, q_norm_w, k_nor
         keep = ctx.enter_context(tc.tile_pool(name="keep", bufs=1))
         work = ctx.enter_context(tc.tile_pool(name="work", bufs=2))
         aux_psum = ctx.enter_context(tc.psum_pool(name="aux_psum", bufs=1))
-        mx_psum = ctx.enter_context(tc.psum_pool(name="mx_psum", bufs=6))
+        mx_psum = ctx.enter_context(tc.psum_pool(name="mx_psum", bufs=MX_BANKS))
         ctx.enter_context(tc.manual_schedule())
 
-        x_tiles, cos_tiles, sin_tiles, w_chunks, w_planes = {}, {}, {}, {}, {}
+        x_tiles, cos_tiles, sin_tiles, w_chunks, w_chunk_scales = {}, {}, {}, {}, {}
 
         def load_rows(dst, src, name, first, count):
             width = src.shape[1]
@@ -68,15 +79,15 @@ def tile_gemmaattention_pa_kernel(tc, hidden, w_words, w_scales, q_norm_w, k_nor
                 w_chunks[first + i] = tile[:, :, 2 * BANK * i:2 * BANK * (i + 1)]
 
         def load_scales(col0, col1):
-            plane = keep.tile([P, PASSES, col1 - col0], U8, name="w_scale_%d" % col0, align_bytes=64)
-            for quad in range(4):
-                src = w_scales[:, 4 * quad:4 * quad + 4, col0:col1].rearrange("g r n -> r g n")
-                nc.sync.dma_start(out=plane[32 * quad:32 * quad + 4, :, :].bitcast(I32), in_=src.bitcast(I32))
-            for c in range(col0 // BANK, col1 // BANK):
-                w_planes[c] = plane[:, :, c * BANK - col0:(c + 1) * BANK - col0]
+            tile = keep.tile([P, PASSES, col1 - col0], U8, name="w_scale_%d" % col0, align_bytes=64)
+            for r in range(4):
+                src = w_scales[:, r:16:4, col0:col1].rearrange("g q n -> q g n")
+                nc.sync.dma_start(out=tile[r:P:32, :, :].bitcast(I32), in_=src.bitcast(I32))
+            for chunk in range(col0 // BANK, col1 // BANK):
+                w_chunk_scales[chunk] = tile[:, :, chunk * BANK - col0:(chunk + 1) * BANK - col0]
 
         norm_row = keep.tile([P, 2, D], BF16)
-        nc.vector.memset(norm_row[:], 0.0)
+        nc.gpsimd.memset(norm_row[:], 0.0)
         ident = keep.tile([P, P], F32)
         make_identity(nc, ident[:])
         ones = keep.tile([P, P], BF16)
@@ -86,146 +97,158 @@ def tile_gemmaattention_pa_kernel(tc, hidden, w_words, w_scales, q_norm_w, k_nor
         nc.scalar.activation(out=warm[:], in_=ones[:, 0:1], func=ACT.Abs_reciprocal_sqrt)
 
         load_rows(x_tiles, hidden, "x", 0, 1)
-        load_scales(0, EARLY_SCALE_COLS)
-        load_weights(0, 2)
+        load_scales(0, NQ)
         nc.sync.dma_start(out=norm_row[0:1, 0, :], in_=q_norm_w.unsqueeze(0))
         nc.sync.dma_start(out=norm_row[0:1, 1, :], in_=k_norm_w.unsqueeze(0))
+        load_weights(0, 2)
         load_rows(cos_tiles, cos, "cos", 0, 2)
         load_rows(sin_tiles, sin, "sin", 0, 2)
         load_rows(x_tiles, hidden, "x", 1, 1)
         load_weights(2, 2)
-        load_scales(EARLY_SCALE_COLS, N_ALL)
-        load_weights(4, 2)
-        load_weights(6, 2)
+        load_weights(Q_STEPS, 2)
+        load_scales(NQ, NQ + NK)
         load_rows(x_tiles, hidden, "x", 2, 2)
         load_rows(cos_tiles, cos, "cos", 2, TILES - 2)
         load_rows(sin_tiles, sin, "sin", 2, TILES - 2)
+        load_scales(NQ + NK, N_ALL)
+        load_weights(TILE_STEPS, 2)
         load_rows(x_tiles, hidden, "x", 4, TILES - 4)
 
         eye_pair = keep.tile([P, 2, P], BF16)
         neg_eye_pair = keep.tile([P, 2, P], BF16)
-        for i in range(2):
-            nc.vector.tensor_copy(out=eye_pair[:, i, :], in_=ident[:])
+        for which in range(2):
+            nc.vector.tensor_copy(out=eye_pair[:, which, :], in_=ident[:])
         nc.vector.tensor_scalar(out=neg_eye_pair[:], in0=eye_pair[:], scalar1=-1.0, scalar2=None, op0=ALU.mult)
 
-        xt_banks, cst_banks, grouped, codes, scales, cs_t, table_banks, tables = {}, {}, {}, {}, {}, {}, {}, {}
+        x_banks, angle_banks, grouped, x_codes, x_scales, angles_t, table_banks, tables = {}, {}, {}, {}, {}, {}, {}, {}
         heads, sums, rstd, products, v_banks, v_tiles = {}, {}, {}, {}, {}, {}
-
         unstored = []
 
         def transpose_x(t):
             words = x_tiles[t].bitcast(F32)
-            xt = aux_psum.tile([P, PASSES, 2, P], F32, name="aux_a")
+            bank = aux_psum.tile([P, PASSES, 2, P], F32, name=AUX_BANKS[0])
             for g in range(PASSES):
                 for u in range(2):
-                    nc.tensor.transpose(xt[:, g, u, :], words[:, 256 * g + u:256 * (g + 1):2], ident[:])
-            xt_banks[t] = xt
+                    nc.tensor.transpose(bank[:, g, u, :], words[:, PASS_WORDS * g + u:PASS_WORDS * (g + 1):2], ident[:])
+            x_banks[t] = bank
 
-        def transpose_cos_sin(t):
-            cst = aux_psum.tile([P, 2, 2, P], BF16, name="aux_b")
+        def transpose_angles(t):
+            bank = aux_psum.tile([P, 2, 2, P], BF16, name=AUX_BANKS[1])
             for i, src in enumerate((cos_tiles[t], sin_tiles[t])):
                 for hf in range(2):
-                    nc.tensor.transpose(cst[:, i, hf, :], src[:, hf * HALF:(hf + 1) * HALF], eye_pair[:, 0, :])
-            cst_banks[t] = cst
+                    nc.tensor.transpose(bank[:, i, hf, :], src[:, hf * HALF:(hf + 1) * HALF], eye_pair[:, 0, :])
+            angle_banks[t] = bank
 
         def copy_x(t, copy):
             tile = work.tile([P, PASSES, P, 2], F32, name="grouped", align_bytes=64)
-            copy(out=tile[:], in_=xt_banks[t][:].rearrange("p g u r -> p g r u"))
+            copy(out=tile[:], in_=x_banks[t][:].rearrange("p g u r -> p g r u"))
             grouped[t] = tile
 
         def quantize_x(t):
-            codes[t] = work.tile([P, PASSES * P], U32, name="codes", bufs=3, align_bytes=64)
-            scales[t] = work.tile([P, PASSES * P], U8, name="scales", bufs=3, align_bytes=64)
+            x_codes[t] = work.tile([P, PASSES * P], U32, name="codes", bufs=3, align_bytes=64)
+            x_scales[t] = work.tile([P, PASSES * P], U8, name="scales", bufs=3, align_bytes=64)
             nc.vector.quantize_mx(
-                out=codes[t][:].bitcast(FP8X4),
-                scales=scales[t][:],
+                out=x_codes[t][:].bitcast(FP8X4),
+                scales=x_scales[t][:],
                 in_=grouped[t][:].rearrange("p g r u -> p (g r u)").bitcast(BF16),
             )
 
-        def copy_cos_sin(t):
-            cs_t[t] = work.tile([P, 2, 2, P], BF16, name="cs_t")
-            nc.scalar.copy(out=cs_t[t][:], in_=cst_banks[t][:])
+        def copy_angles(t):
+            angles_t[t] = work.tile([P, 2, 2, P], BF16, name="cs_t")
+            nc.scalar.copy(out=angles_t[t][:], in_=angle_banks[t][:])
 
         def multiply_tables(t):
-            for i, tag in enumerate(("aux_a", "aux_b")):
-                bank = aux_psum.tile([P, 2, 2 * P], F32, name=tag)
+            for i, name in enumerate(AUX_BANKS):
+                bank = aux_psum.tile([P, 2, 2 * P], F32, name=name)
                 for hf in range(2):
-                    gain, one = table_factors[i][hf]
-                    angles = cs_t[t][:, i, hf if i == 0 else 1 - hf, :]
-                    nc.tensor.matmul(bank[:, hf, :], lhsT=angles, rhs=gain, start=True, stop=False)
-                    nc.tensor.matmul(bank[:, hf, :], lhsT=angles, rhs=one, start=False, stop=True)
+                    weight, one = table_factors[i][hf]
+                    angle = angles_t[t][:, i, hf if i == 0 else 1 - hf, :]
+                    nc.tensor.matmul(bank[:, hf, :], lhsT=angle, rhs=weight, start=True, stop=False)
+                    nc.tensor.matmul(bank[:, hf, :], lhsT=angle, rhs=one, start=False, stop=True)
                 table_banks[t, i] = bank
+
+        def new_table(t):
+            tables[t] = work.tile([P, 2, 2, 2, HALF], F32, name="table", bufs=3)
 
         def copy_table(t, i):
             if i == 0:
-                tables[t] = work.tile([P, 2, 2, 2, HALF], F32, name="table", bufs=3)
-            nc.scalar.copy(out=tables[t][:, i, :, :, :].rearrange("p a b c -> p (a b c)"), in_=table_banks[t, i][:].rearrange("p a b -> p (a b)"))
+                new_table(t)
+            nc.scalar.copy(out=tables[t][:, i, :, :, :].rearrange("p a b c -> p (a b c)"), in_=flat(table_banks[t, i][:]))
 
         def project(bank, t, chunk, col0=0, col1=BANK):
             for g in range(PASSES):
                 nc.tensor.matmul_mx(
                     out=bank[:],
-                    lhsT=codes[t][:, g * P:(g + 1) * P].bitcast(FP8X4),
-                    lhsT_scale=scales[t][:, g * P:(g + 1) * P],
+                    lhsT=x_codes[t][:, g * P:(g + 1) * P].bitcast(FP8X4),
+                    lhsT_scale=x_scales[t][:, g * P:(g + 1) * P],
                     rhs=w_chunks[chunk][:, g, 2 * col0:2 * col1].bitcast(FP4X4),
-                    rhs_scale=w_planes[chunk][:, g, col0:col1],
+                    rhs_scale=w_chunk_scales[chunk][:, g, col0:col1],
                     start=(g == 0),
                     stop=(g == PASSES - 1),
                 )
-            return bank
 
-        def project_rope_bank(s):
-            t, chunk = divmod(s, ROPE_BANKS)
+        def project_step(s):
+            t, chunk = divmod(s, TILE_STEPS)
             if s == 0:
                 heads[s] = []
                 for h in range(2):
                     bank = mx_psum.tile([P, D], F32, name="mx_bank")
-                    heads[s].append(project(bank, t, chunk, h * D, (h + 1) * D)[:])
+                    project(bank, t, chunk, h * D, (h + 1) * D)
+                    heads[s].append(bank[:])
             else:
                 bank = mx_psum.tile([P, BANK], F32, name="mx_bank")
                 project(bank, t, chunk)
                 heads[s] = [bank[:, :D], bank[:, D:]]
 
         def square_sum(s, h):
-            unit, col = s // UNIT, 2 * (s % UNIT) + h
-            if col == 0:
-                sums[unit] = work.tile([P, 2 * UNIT], F32, name="sums", bufs=3)
-                rstd[unit] = work.tile([P, 2 * UNIT], F32, name="rstd", bufs=3)
+            unit, head = s // UNIT, 2 * (s % UNIT) + h
+            if head == 0:
+                sums[unit] = work.tile([P, UNIT_HEADS], F32, name="sums", bufs=3)
+                rstd[unit] = work.tile([P, UNIT_HEADS], F32, name="rstd", bufs=3)
             squares = work.tile([P, D], BF16, name="squares")
-            nc.scalar.activation(out=squares[:], in_=heads[s][h], func=ACT.Square, accum_out=sums[unit][:, col:col + 1])
+            nc.scalar.activation(out=squares[:], in_=heads[s][h], func=ACT.Square, accum_out=sums[unit][:, head:head + 1])
 
-        def inverse_rms(unit, col0, col1):
-            nc.scalar.activation(out=rstd[unit][:, col0:col1], in_=sums[unit][:, col0:col1], func=ACT.Abs_reciprocal_sqrt, scale=1.0 / D, bias=EPS)
+        def inverse_rms(unit, head0, head1):
+            nc.scalar.activation(
+                out=rstd[unit][:, head0:head1], in_=sums[unit][:, head0:head1],
+                func=ACT.Abs_reciprocal_sqrt, scale=1.0 / D, bias=EPS,
+            )
 
         def rope_products(s, h):
-            t, j = divmod(s, ROPE_BANKS)
-            unit, col = s // UNIT, 2 * (s % UNIT) + h
-            if col == 0:
-                products[unit] = work.tile([P, 2 * UNIT, 2, 2, HALF], F32, name="products", bufs=3)
-            head = heads[s][h].rearrange("p (a b) -> p a b", a=2)
+            t, chunk = divmod(s, TILE_STEPS)
+            unit, head = s // UNIT, 2 * (s % UNIT) + h
+            if head == 0:
+                products[unit] = work.tile([P, UNIT_HEADS, 2, 2, HALF], F32, name="products", bufs=3)
+            halves = heads[s][h].rearrange("p (a b) -> p a b", a=2)
             nc.vector.scalar_tensor_tensor(
-                out=products[unit][:, col, :, :, :],
-                in0=head.unsqueeze(1).broadcast_to([P, 2, 2, HALF]),
-                scalar=rstd[unit][:, col:col + 1],
-                in1=tables[t][:, :, :, 0 if j < Q_BANKS else 1, :],
+                out=products[unit][:, head, :, :, :],
+                in0=halves.unsqueeze(1).broadcast_to([P, 2, 2, HALF]),
+                scalar=rstd[unit][:, head:head + 1],
+                in1=tables[t][:, :, :, 0 if chunk < Q_STEPS else 1, :],
                 op0=ALU.mult,
                 op1=ALU.mult,
             )
 
         def add_products(engine, unit, head0, head1):
             y = work.tile([P, head1 - head0, 2, HALF], F32, name="y", bufs=6)
-            engine.tensor_tensor(out=y[:], in0=products[unit][:, head0:head1, 0, :, :], in1=products[unit][:, head0:head1, 1, ::-1, :], op=ALU.add)
+            engine.tensor_tensor(
+                out=y[:], in0=products[unit][:, head0:head1, 0, :, :],
+                in1=products[unit][:, head0:head1, 1, ::-1, :], op=ALU.add,
+            )
             unstored.append((y, unit, head0, head1))
 
         def store_oldest():
             y, unit, head0, head1 = unstored.pop(0)
-            t, j = divmod(unit * UNIT, ROPE_BANKS)
-            dst, first = (q_rows, j * BANK) if j < Q_BANKS else (k_rows, (j - Q_BANKS) * BANK)
-            nc.sync.dma_start(out=dst[t * P:(t + 1) * P, first + head0 * D:first + head1 * D], in_=y[:].rearrange("p h a b -> p (h a b)"))
+            t, chunk = divmod(unit * UNIT, TILE_STEPS)
+            dst, first = (q_rows, chunk * BANK) if chunk < Q_STEPS else (k_rows, (chunk - Q_STEPS) * BANK)
+            nc.sync.dma_start(
+                out=dst[t * P:(t + 1) * P, first + head0 * D:first + head1 * D],
+                in_=y[:].rearrange("p h a b -> p (h a b)"),
+            )
 
         def project_v(t, i):
-            bank = aux_psum.tile([P, BANK], F32, name=("aux_a", "aux_b")[i])
-            v_banks[t, i] = project(bank, t, ROPE_BANKS + i)
+            v_banks[t, i] = aux_psum.tile([P, BANK], F32, name=AUX_BANKS[i])
+            project(v_banks[t, i], t, TILE_STEPS + i)
 
         def copy_v(t, i):
             if i == 0:
@@ -237,92 +260,93 @@ def tile_gemmaattention_pa_kernel(tc, hidden, w_words, w_scales, q_norm_w, k_nor
         transpose_x(0)
         copy_x(0, nc.scalar.copy)
         norm_bank = mx_psum.tile([P, 2, 2, HALF], F32, name="mx_bank")
-        nc.tensor.matmul(norm_bank[:].rearrange("p a b c -> p (a b c)"), lhsT=ones[:], rhs=norm_row[:].rearrange("p a d -> p (a d)"), start=True, stop=True)
+        nc.tensor.matmul(norm_bank[:].rearrange("p a b c -> p (a b c)"), lhsT=ones[:], rhs=flat(norm_row[:]), start=True, stop=True)
         quantize_x(0)
         norm_all = keep.tile([P, 2, 2, HALF], BF16)
         nc.scalar.copy(out=norm_all[:], in_=norm_bank[:])
         neg_sin = keep.tile([P, HALF], BF16)
-        nc.scalar.activation(out=neg_sin[:], in_=sin_tiles[0][:, :HALF], func=ACT.Copy, scale=-1.0)
         diag = keep.tile([P, 2, 2, HALF], BF16)
         neg_diag = keep.tile([P, 2, HALF], BF16)
         for hf in range(2):
             nc.gpsimd.tensor_tensor(out=diag[:, hf, :, :], in0=norm_all[:, :, hf, :], in1=eye_pair[:], op=ALU.mult)
         nc.gpsimd.tensor_tensor(out=neg_diag[:], in0=norm_all[:, :, 1, :], in1=neg_eye_pair[:], op=ALU.mult)
-        flat = lambda ap: ap.rearrange("p a b -> p (a b)")
         plus, minus = flat(eye_pair[:]), flat(neg_eye_pair[:])
         table_factors = (
             ((flat(diag[:, 0, :, :]), plus), (flat(diag[:, 1, :, :]), plus)),
             ((flat(diag[:, 0, :, :]), plus), (flat(neg_diag[:]), minus)),
         )
-        tables[0] = work.tile([P, 2, 2, 2, HALF], F32, name="table", bufs=3)
+        new_table(0)
 
-        def first_tables(which):
+        def first_table(which):
             parts = (
                 (tables[0][:, 0, :, which, :], norm_bank[:, which, :, :], cos_tiles[0].rearrange("p (a b) -> p a b", a=2)),
                 (tables[0][:, 1, 0, which, :], norm_bank[:, which, 0, :], sin_tiles[0][:, HALF:]),
                 (tables[0][:, 1, 1, which, :], norm_bank[:, which, 1, :], neg_sin[:]),
             )
-            for dst, weight, angles in parts:
-                nc.vector.scalar_tensor_tensor(out=dst, in0=weight, scalar=1.0, in1=angles, op0=ALU.add, op1=ALU.mult)
+            for dst, weight, angle in parts:
+                nc.vector.scalar_tensor_tensor(out=dst, in0=weight, scalar=1.0, in1=angle, op0=ALU.add, op1=ALU.mult)
 
-        first_tables(0)
-        for s in range(MM_LEAD):
+        nc.scalar.activation(out=neg_sin[:], in_=sin_tiles[0][:, :HALF], func=ACT.Copy, scale=-1.0)
+        first_table(0)
+        for s in range(MATMUL_LEAD):
             if s == UNIT:
                 transpose_x(1)
-                transpose_cos_sin(1)
-            project_rope_bank(s)
-        for col in range(2 * UNIT):
-            square_sum(col // 2, col % 2)
-            if col in (0, 1):
-                inverse_rms(0, col, col + 1)
-        inverse_rms(0, 2, 2 * UNIT)
+                transpose_angles(1)
+            project_step(s)
+        for head in range(UNIT_HEADS):
+            square_sum(head // 2, head % 2)
+            if head < 2:
+                inverse_rms(0, head, head + 1)
+        inverse_rms(0, 2, UNIT_HEADS)
 
-        steps = TILES * ROPE_BANKS
-        prep_start = {max(u * ROPE_BANKS - PREP_LEAD, 0): u for u in range(1, TILES)}
-        v_start = {min(t * ROPE_BANKS + V_STEP, steps - V_END - 2 * (TILES - 1 - t)): t for t in range(TILES)}
-        for s in range(steps):
+        prep_start = {max(t * TILE_STEPS - PREP_LEAD, 0): t for t in range(1, TILES)}
+        v_start = {min(t * TILE_STEPS + V_DELAY, STEPS - V_END - 2 * (TILES - 1 - t)): t for t in range(TILES)}
+        for s in range(STEPS):
             if s in prep_start and s > 0:
                 transpose_x(prep_start[s])
-                transpose_cos_sin(prep_start[s])
+                transpose_angles(prep_start[s])
             if s - 2 in prep_start:
                 multiply_tables(prep_start[s - 2])
             for i in range(2):
                 if s - i in v_start:
                     project_v(v_start[s - i], i)
-            if s + MM_LEAD < steps:
-                project_rope_bank(s + MM_LEAD)
-            ahead = s + SQ_LEAD
-            if ahead < steps:
+            if s + MATMUL_LEAD < STEPS:
+                project_step(s + MATMUL_LEAD)
+
+            ahead = s + SQUARE_LEAD
+            if ahead < STEPS:
                 for h in range(2):
                     square_sum(ahead, h)
             if s in prep_start and s > 0:
                 copy_x(prep_start[s], nc.scalar.copy)
             if s - 1 in prep_start:
-                copy_cos_sin(prep_start[s - 1])
+                copy_angles(prep_start[s - 1])
             for i in range(2):
                 if s - 2 - i in prep_start:
                     copy_table(prep_start[s - 2 - i], i)
                 if s - i in v_start:
                     copy_v(v_start[s - i], i)
-            if ahead < steps and ahead % UNIT == UNIT - 1:
-                inverse_rms(ahead // UNIT, 0, 2 * UNIT)
+            if ahead < STEPS and ahead % UNIT == UNIT - 1:
+                inverse_rms(ahead // UNIT, 0, UNIT_HEADS)
+
             rope_products(s, 0)
             if s == 1:
                 quantize_x(1)
             rope_products(s, 1)
             if s == 0:
                 copy_x(1, nc.vector.tensor_copy)
-                first_tables(1)
+                first_table(1)
             if s - 1 in prep_start and s > 1:
                 quantize_x(prep_start[s - 1])
+
             if s % UNIT == UNIT - 1:
-                if s < steps - 1 - UNIT:
-                    add_products(nc.gpsimd, s // UNIT, 0, 2 * UNIT)
+                if s < STEPS - 1 - UNIT:
+                    add_products(nc.gpsimd, s // UNIT, 0, UNIT_HEADS)
                     if len(unstored) > STORE_LAG:
                         store_oldest()
-                elif s < steps - 1:
-                    for b in range(UNIT):
-                        add_products(nc.gpsimd, s // UNIT, 2 * b, 2 * b + 2)
+                elif s < STEPS - 1:
+                    for head0, head1 in ((0, 2), (2, 4)):
+                        add_products(nc.gpsimd, s // UNIT, head0, head1)
                 else:
                     for head0, head1 in ((0, 2), (2, 3), (3, 4)):
                         add_products(nc.vector, s // UNIT, head0, head1)

from contextlib import ExitStack

import concourse.mybir as mybir
from concourse.masks import make_identity

S, HID, H, KV, D = 1024, 1024, 8, 4, 256
NQ, NK = H * D, KV * D
N_ALL = NQ + 2 * NK
EPS = 1e-6
FLOPS = 2 * S * HID * N_ALL

F32 = mybir.dt.float32
BF16 = mybir.dt.bfloat16
I32 = mybir.dt.int32
U32 = mybir.dt.uint32
U8 = mybir.dt.uint8
FP8X4 = mybir.dt.float8_e5m2_x4
FP4X4 = mybir.dt.float4_e2m1fn_x4
ALU = mybir.AluOpType
ACT = mybir.ActivationFunctionType

P = 128
HALF = D // 2
K_PASS = 512
PASSES = HID // K_PASS
PASS_WORDS = K_PASS // 2
BANK = 512
TILES = S // P
TILE_STEPS = (NQ + NK) // BANK
Q_STEPS = NQ // BANK
STEPS = TILES * TILE_STEPS
UNIT = 2
UNIT_HEADS = 2 * UNIT

SQUARE_LEAD = 2
MATMUL_LEAD = 4
PREP_LEAD = 8
V_DELAY = 8
V_END = 4
STORE_LAG = 1

MX_BANKS = 6
AUX_BANKS = ("aux_a", "aux_b")


def flat(ap):
    return ap.rearrange("p a b -> p (a b)")


def tile_gemmaattention_pa_kernel(tc, hidden, w_words, w_scales, q_norm_w, k_norm_w, cos, sin, out_q, out_k, out_v):
    nc = tc.nc
    q_rows = out_q.rearrange("s h d -> s (h d)")
    k_rows = out_k.rearrange("s h d -> s (h d)")
    v_rows = out_v.rearrange("s h d -> s (h d)")
    w_by_partition = w_words.rearrange("g p n -> p g n")

    with ExitStack() as ctx:
        keep = ctx.enter_context(tc.tile_pool(name="keep", bufs=1))
        work = ctx.enter_context(tc.tile_pool(name="work", bufs=2))
        aux_psum = ctx.enter_context(tc.psum_pool(name="aux_psum", bufs=1))
        mx_psum = ctx.enter_context(tc.psum_pool(name="mx_psum", bufs=MX_BANKS))
        ctx.enter_context(tc.manual_schedule())

        x_tiles, cos_tiles, sin_tiles, w_chunks, w_chunk_scales = {}, {}, {}, {}, {}

        def load_rows(dst, src, name, first, count):
            width = src.shape[1]
            tile = keep.tile([P, count, width], BF16, name="%s_%d" % (name, first))
            rows = src[first * P:(first + count) * P, :]
            nc.sync.dma_start(out=tile[:], in_=rows.rearrange("(t p) w -> p t w", p=P))
            for i in range(count):
                dst[first + i] = tile[:, i, :]

        def load_weights(first, count):
            tile = keep.tile([P, PASSES, 2 * BANK * count], U8, name="w_%d" % first, align_bytes=64)
            src = w_by_partition[:, :, 2 * BANK * first:2 * BANK * (first + count)]
            nc.sync.dma_start(out=tile[:].bitcast(I32), in_=src.bitcast(I32))
            for i in range(count):
                w_chunks[first + i] = tile[:, :, 2 * BANK * i:2 * BANK * (i + 1)]

        def load_scales(col0, col1):
            tile = keep.tile([P, PASSES, col1 - col0], U8, name="w_scale_%d" % col0, align_bytes=64)
            for r in range(4):
                src = w_scales[:, r:16:4, col0:col1].rearrange("g q n -> q g n")
                nc.sync.dma_start(out=tile[r:P:32, :, :].bitcast(I32), in_=src.bitcast(I32))
            for chunk in range(col0 // BANK, col1 // BANK):
                w_chunk_scales[chunk] = tile[:, :, chunk * BANK - col0:(chunk + 1) * BANK - col0]

        norm_row = keep.tile([P, 2, D], BF16)
        nc.gpsimd.memset(norm_row[:], 0.0)
        ident = keep.tile([P, P], F32)
        make_identity(nc, ident[:])
        ones = keep.tile([P, P], BF16)
        nc.vector.memset(ones[:], 1.0)

        warm = keep.tile([P, 1], F32)
        nc.scalar.activation(out=warm[:], in_=ones[:, 0:1], func=ACT.Abs_reciprocal_sqrt)

        load_rows(x_tiles, hidden, "x", 0, 1)
        load_scales(0, NQ)
        nc.sync.dma_start(out=norm_row[0:1, 0, :], in_=q_norm_w.unsqueeze(0))
        nc.sync.dma_start(out=norm_row[0:1, 1, :], in_=k_norm_w.unsqueeze(0))
        load_weights(0, 2)
        load_rows(cos_tiles, cos, "cos", 0, 2)
        load_rows(sin_tiles, sin, "sin", 0, 2)
        load_rows(x_tiles, hidden, "x", 1, 1)
        load_weights(2, 2)
        load_weights(Q_STEPS, 2)
        load_scales(NQ, NQ + NK)
        load_rows(x_tiles, hidden, "x", 2, 2)
        load_rows(cos_tiles, cos, "cos", 2, TILES - 2)
        load_rows(sin_tiles, sin, "sin", 2, TILES - 2)
        load_scales(NQ + NK, N_ALL)
        load_weights(TILE_STEPS, 2)
        load_rows(x_tiles, hidden, "x", 4, TILES - 4)

        eye_pair = keep.tile([P, 2, P], BF16)
        neg_eye_pair = keep.tile([P, 2, P], BF16)
        for which in range(2):
            nc.vector.tensor_copy(out=eye_pair[:, which, :], in_=ident[:])
        nc.vector.tensor_scalar(out=neg_eye_pair[:], in0=eye_pair[:], scalar1=-1.0, scalar2=None, op0=ALU.mult)

        x_banks, angle_banks, grouped, x_codes, x_scales, angles_t, table_banks, tables = {}, {}, {}, {}, {}, {}, {}, {}
        heads, sums, rstd, products, v_banks, v_tiles = {}, {}, {}, {}, {}, {}
        unstored = []

        def transpose_x(t):
            words = x_tiles[t].bitcast(F32)
            bank = aux_psum.tile([P, PASSES, 2, P], F32, name=AUX_BANKS[0])
            for g in range(PASSES):
                for u in range(2):
                    nc.tensor.transpose(bank[:, g, u, :], words[:, PASS_WORDS * g + u:PASS_WORDS * (g + 1):2], ident[:])
            x_banks[t] = bank

        def transpose_angles(t):
            bank = aux_psum.tile([P, 2, 2, P], BF16, name=AUX_BANKS[1])
            for i, src in enumerate((cos_tiles[t], sin_tiles[t])):
                for hf in range(2):
                    nc.tensor.transpose(bank[:, i, hf, :], src[:, hf * HALF:(hf + 1) * HALF], eye_pair[:, 0, :])
            angle_banks[t] = bank

        def copy_x(t, copy):
            tile = work.tile([P, PASSES, P, 2], F32, name="grouped", align_bytes=64)
            copy(out=tile[:], in_=x_banks[t][:].rearrange("p g u r -> p g r u"))
            grouped[t] = tile

        def quantize_x(t):
            x_codes[t] = work.tile([P, PASSES * P], U32, name="codes", bufs=3, align_bytes=64)
            x_scales[t] = work.tile([P, PASSES * P], U8, name="scales", bufs=3, align_bytes=64)
            nc.vector.quantize_mx(
                out=x_codes[t][:].bitcast(FP8X4),
                scales=x_scales[t][:],
                in_=grouped[t][:].rearrange("p g r u -> p (g r u)").bitcast(BF16),
            )

        def copy_angles(t):
            angles_t[t] = work.tile([P, 2, 2, P], BF16, name="cs_t")
            nc.scalar.copy(out=angles_t[t][:], in_=angle_banks[t][:])

        def multiply_tables(t):
            for i, name in enumerate(AUX_BANKS):
                bank = aux_psum.tile([P, 2, 2 * P], F32, name=name)
                for hf in range(2):
                    weight, one = table_factors[i][hf]
                    angle = angles_t[t][:, i, hf if i == 0 else 1 - hf, :]
                    nc.tensor.matmul(bank[:, hf, :], lhsT=angle, rhs=weight, start=True, stop=False)
                    nc.tensor.matmul(bank[:, hf, :], lhsT=angle, rhs=one, start=False, stop=True)
                table_banks[t, i] = bank

        def new_table(t):
            tables[t] = work.tile([P, 2, 2, 2, HALF], F32, name="table", bufs=3)

        def copy_table(t, i):
            if i == 0:
                new_table(t)
            nc.scalar.copy(out=tables[t][:, i, :, :, :].rearrange("p a b c -> p (a b c)"), in_=flat(table_banks[t, i][:]))

        def project(bank, t, chunk, col0=0, col1=BANK):
            for g in range(PASSES):
                nc.tensor.matmul_mx(
                    out=bank[:],
                    lhsT=x_codes[t][:, g * P:(g + 1) * P].bitcast(FP8X4),
                    lhsT_scale=x_scales[t][:, g * P:(g + 1) * P],
                    rhs=w_chunks[chunk][:, g, 2 * col0:2 * col1].bitcast(FP4X4),
                    rhs_scale=w_chunk_scales[chunk][:, g, col0:col1],
                    start=(g == 0),
                    stop=(g == PASSES - 1),
                )

        def project_step(s):
            t, chunk = divmod(s, TILE_STEPS)
            if s == 0:
                heads[s] = []
                for h in range(2):
                    bank = mx_psum.tile([P, D], F32, name="mx_bank")
                    project(bank, t, chunk, h * D, (h + 1) * D)
                    heads[s].append(bank[:])
            else:
                bank = mx_psum.tile([P, BANK], F32, name="mx_bank")
                project(bank, t, chunk)
                heads[s] = [bank[:, :D], bank[:, D:]]

        def square_sum(s, h):
            unit, head = s // UNIT, 2 * (s % UNIT) + h
            if head == 0:
                sums[unit] = work.tile([P, UNIT_HEADS], F32, name="sums", bufs=3)
                rstd[unit] = work.tile([P, UNIT_HEADS], F32, name="rstd", bufs=3)
            squares = work.tile([P, D], BF16, name="squares")
            nc.scalar.activation(out=squares[:], in_=heads[s][h], func=ACT.Square, accum_out=sums[unit][:, head:head + 1])

        def inverse_rms(unit, head0, head1):
            nc.scalar.activation(
                out=rstd[unit][:, head0:head1], in_=sums[unit][:, head0:head1],
                func=ACT.Abs_reciprocal_sqrt, scale=1.0 / D, bias=EPS,
            )

        def rope_products(s, h):
            t, chunk = divmod(s, TILE_STEPS)
            unit, head = s // UNIT, 2 * (s % UNIT) + h
            if head == 0:
                products[unit] = work.tile([P, UNIT_HEADS, 2, 2, HALF], F32, name="products", bufs=3)
            halves = heads[s][h].rearrange("p (a b) -> p a b", a=2)
            nc.vector.scalar_tensor_tensor(
                out=products[unit][:, head, :, :, :],
                in0=halves.unsqueeze(1).broadcast_to([P, 2, 2, HALF]),
                scalar=rstd[unit][:, head:head + 1],
                in1=tables[t][:, :, :, 0 if chunk < Q_STEPS else 1, :],
                op0=ALU.mult,
                op1=ALU.mult,
            )

        def add_products(engine, unit, head0, head1):
            y = work.tile([P, head1 - head0, 2, HALF], F32, name="y", bufs=6)
            engine.tensor_tensor(
                out=y[:], in0=products[unit][:, head0:head1, 0, :, :],
                in1=products[unit][:, head0:head1, 1, ::-1, :], op=ALU.add,
            )
            unstored.append((y, unit, head0, head1))

        def store_oldest():
            y, unit, head0, head1 = unstored.pop(0)
            t, chunk = divmod(unit * UNIT, TILE_STEPS)
            dst, first = (q_rows, chunk * BANK) if chunk < Q_STEPS else (k_rows, (chunk - Q_STEPS) * BANK)
            nc.sync.dma_start(
                out=dst[t * P:(t + 1) * P, first + head0 * D:first + head1 * D],
                in_=y[:].rearrange("p h a b -> p (h a b)"),
            )

        def project_v(t, i):
            v_banks[t, i] = aux_psum.tile([P, BANK], F32, name=AUX_BANKS[i])
            project(v_banks[t, i], t, TILE_STEPS + i)

        def copy_v(t, i):
            if i == 0:
                v_tiles[t] = work.tile([P, NK], F32, name="v_tile", bufs=3)
            nc.scalar.copy(out=v_tiles[t][:, i * BANK:(i + 1) * BANK], in_=v_banks[t, i][:])
            if i == 1:
                nc.sync.dma_start(out=v_rows[t * P:(t + 1) * P, :], in_=v_tiles[t][:])

        transpose_x(0)
        copy_x(0, nc.scalar.copy)
        norm_bank = mx_psum.tile([P, 2, 2, HALF], F32, name="mx_bank")
        nc.tensor.matmul(norm_bank[:].rearrange("p a b c -> p (a b c)"), lhsT=ones[:], rhs=flat(norm_row[:]), start=True, stop=True)
        quantize_x(0)
        norm_all = keep.tile([P, 2, 2, HALF], BF16)
        nc.scalar.copy(out=norm_all[:], in_=norm_bank[:])
        neg_sin = keep.tile([P, HALF], BF16)
        diag = keep.tile([P, 2, 2, HALF], BF16)
        neg_diag = keep.tile([P, 2, HALF], BF16)
        for hf in range(2):
            nc.gpsimd.tensor_tensor(out=diag[:, hf, :, :], in0=norm_all[:, :, hf, :], in1=eye_pair[:], op=ALU.mult)
        nc.gpsimd.tensor_tensor(out=neg_diag[:], in0=norm_all[:, :, 1, :], in1=neg_eye_pair[:], op=ALU.mult)
        plus, minus = flat(eye_pair[:]), flat(neg_eye_pair[:])
        table_factors = (
            ((flat(diag[:, 0, :, :]), plus), (flat(diag[:, 1, :, :]), plus)),
            ((flat(diag[:, 0, :, :]), plus), (flat(neg_diag[:]), minus)),
        )
        new_table(0)

        def first_table(which):
            parts = (
                (tables[0][:, 0, :, which, :], norm_bank[:, which, :, :], cos_tiles[0].rearrange("p (a b) -> p a b", a=2)),
                (tables[0][:, 1, 0, which, :], norm_bank[:, which, 0, :], sin_tiles[0][:, HALF:]),
                (tables[0][:, 1, 1, which, :], norm_bank[:, which, 1, :], neg_sin[:]),
            )
            for dst, weight, angle in parts:
                nc.vector.scalar_tensor_tensor(out=dst, in0=weight, scalar=1.0, in1=angle, op0=ALU.add, op1=ALU.mult)

        nc.scalar.activation(out=neg_sin[:], in_=sin_tiles[0][:, :HALF], func=ACT.Copy, scale=-1.0)
        first_table(0)
        for s in range(MATMUL_LEAD):
            if s == UNIT:
                transpose_x(1)
                transpose_angles(1)
            project_step(s)
        for head in range(UNIT_HEADS):
            square_sum(head // 2, head % 2)
            if head < 2:
                inverse_rms(0, head, head + 1)
        inverse_rms(0, 2, UNIT_HEADS)

        prep_start = {max(t * TILE_STEPS - PREP_LEAD, 0): t for t in range(1, TILES)}
        v_start = {min(t * TILE_STEPS + V_DELAY, STEPS - V_END - 2 * (TILES - 1 - t)): t for t in range(TILES)}
        for s in range(STEPS):
            if s in prep_start and s > 0:
                transpose_x(prep_start[s])
                transpose_angles(prep_start[s])
            if s - 2 in prep_start:
                multiply_tables(prep_start[s - 2])
            for i in range(2):
                if s - i in v_start:
                    project_v(v_start[s - i], i)
            if s + MATMUL_LEAD < STEPS:
                project_step(s + MATMUL_LEAD)

            ahead = s + SQUARE_LEAD
            if ahead < STEPS:
                for h in range(2):
                    square_sum(ahead, h)
            if s in prep_start and s > 0:
                copy_x(prep_start[s], nc.scalar.copy)
            if s - 1 in prep_start:
                copy_angles(prep_start[s - 1])
            for i in range(2):
                if s - 2 - i in prep_start:
                    copy_table(prep_start[s - 2 - i], i)
                if s - i in v_start:
                    copy_v(v_start[s - i], i)
            if ahead < STEPS and ahead % UNIT == UNIT - 1:
                inverse_rms(ahead // UNIT, 0, UNIT_HEADS)

            rope_products(s, 0)
            if s == 1:
                quantize_x(1)
            rope_products(s, 1)
            if s == 0:
                copy_x(1, nc.vector.tensor_copy)
                first_table(1)
            if s - 1 in prep_start and s > 1:
                quantize_x(prep_start[s - 1])

            if s % UNIT == UNIT - 1:
                if s < STEPS - 1 - UNIT:
                    add_products(nc.gpsimd, s // UNIT, 0, UNIT_HEADS)
                    if len(unstored) > STORE_LAG:
                        store_oldest()
                elif s < STEPS - 1:
                    for head0, head1 in ((0, 2), (2, 4)):
                        add_products(nc.gpsimd, s // UNIT, head0, head1)
                else:
                    for head0, head1 in ((0, 2), (2, 3), (3, 4)):
                        add_products(nc.vector, s // UNIT, head0, head1)
        while unstored:
            store_oldest()
